import numpy as np
import ml_dtypes


def mxq(x, axis, fmt="e4m3"):
    dtype, down = {"e4m3": (ml_dtypes.float8_e4m3fn, 7), "e5m2": (ml_dtypes.float8_e5m2, 14)}[fmt]
    v = np.moveaxis(np.asarray(x, np.float32).astype(ml_dtypes.bfloat16).astype(np.float64), axis, -1)
    blocks = v.reshape(v.shape[:-1] + (-1, 32))
    amax = np.abs(blocks).max(-1, keepdims=True)
    byte = np.maximum(np.where(amax > 0, np.frexp(amax)[1] - 1 + 127, 0) - down, 1)
    scale = np.exp2(byte - 127.0)
    codes = (blocks / scale).astype(np.float32).astype(dtype).astype(np.float64)
    return np.moveaxis((codes * scale).reshape(v.shape), -1, axis)


WIDE = False


def mx_kscale(k):
    if not WIDE:
        return np.ones(k)
    levels = np.array([10, -10, 5, -5, 0])
    a = np.random.permutation(np.resize(levels, k // 512 * 4)).reshape(k // 512, 4)
    idx = np.arange(k)
    return np.exp2(a[idx // 512, idx % 128 // 32])


BF16 = ml_dtypes.bfloat16


def bf(x):
    return np.asarray(x, np.float32).astype(BF16)


def f64(x):
    return np.asarray(x).astype(np.float64)


E2M1 = np.array([0.0, 0.5, 1.0, 1.5, 2.0, 3.0, 4.0, 6.0, -0.0, -0.5, -1.0, -1.5, -2.0, -3.0, -4.0, -6.0])


def pack_weight(w, fmt):
    k, n = w.shape
    w = f64(bf(w)).reshape(k // 32, 32, n)
    amax = np.abs(w).max(1)
    if fmt == "e4m3":
        byte = np.frexp(amax)[1] - 1 + 127 - 7
    else:
        mant, ex = np.frexp(amax / 6.0)
        byte = np.where(mant > 0.5, ex, ex - 1) + 127
    byte = np.clip(np.where(amax > 0, byte, 1), 1, 254)
    scaled = (w * np.exp2(127.0 - byte)[:, None, :]).reshape(k, n).astype(np.float32)
    by_word = np.ascontiguousarray(scaled.reshape(k // 512, 128, 4, n).transpose(0, 1, 3, 2))
    if fmt == "e4m3":
        words = by_word.astype(ml_dtypes.float8_e4m3fn).view(np.uint8)
    else:
        c = by_word.astype(ml_dtypes.float4_e2m1fn).view(np.uint8) & 0xF
        words = c[..., 0::2] | (c[..., 1::2] << 4)
    return np.ascontiguousarray(words), np.ascontiguousarray(byte.astype(np.uint8).reshape(k // 512, 16, n))


def unpack_weight(words, scales, fmt):
    g, p, n, _ = words.shape
    if fmt == "e4m3":
        vals = np.ascontiguousarray(words).view(ml_dtypes.float8_e4m3fn).astype(np.float64)
    else:
        nib = np.empty((g, p, n, 4), np.uint8)
        nib[..., 0::2] = words & 0xF
        nib[..., 1::2] = words >> 4
        vals = E2M1[nib]
    vals = vals * np.repeat(np.exp2(scales.astype(np.float64) - 127.0), 8, axis=1)[..., None]
    return vals.transpose(0, 1, 3, 2).reshape(g * 512, n)


B, IN, HID, BLK, OUT = 512, 1024, 4096, 512, 10
NB = HID // BLK


def setup_inputs():
    s = mx_kscale(IN)
    t = np.tile(mx_kscale(BLK), NB)
    x = bf(np.random.standard_normal((B, IN)) * s)
    W1 = np.random.standard_normal((HID, IN)) / np.sqrt(IN) / s * t[:, None]
    W1_words, W1_scales = pack_weight(np.ascontiguousarray(W1.T), "e4m3")
    return {
        "x": x,
        "W1_words": W1_words,
        "W1_scales": W1_scales,
        "b1": bf(np.random.standard_normal(HID) * 0.3 * t),
        "Wb": bf(np.random.standard_normal((NB, BLK, BLK)) * 1.4 / np.sqrt(BLK) / t.reshape(NB, 1, BLK)),
        "bb": bf(np.random.standard_normal(HID) * 0.3),
    }


def reference(x, W1_words, W1_scales, b1, Wb, bb):
    h = np.maximum((mxq(f64(x), 1, "e4m3") @ unpack_weight(W1_words, W1_scales, "e4m3")) + f64(b1), 0.0)
    hb = h.reshape(B, NB, BLK)
    yb = (mxq(hb, 2, "e4m3").transpose(1, 0, 2) @ mxq(f64(Wb), 2, "e4m3").transpose(0, 2, 1)).transpose(1, 0, 2)
    return np.maximum(yb.reshape(B, HID) + f64(bb), 0.0)

@@ -1,0 +1,211 @@
+from contextlib import ExitStack
+
+import concourse.mybir as mybir
+from concourse.masks import make_identity
+
+F32 = mybir.dt.float32
+BF16 = mybir.dt.bfloat16
+I32 = mybir.dt.int32
+U32 = mybir.dt.uint32
+U8 = mybir.dt.uint8
+FP8X4 = mybir.dt.float8_e4m3fn_x4
+RELU = mybir.ActivationFunctionType.Relu
+ADD = mybir.AluOpType.add
+MAX = mybir.AluOpType.max
+
+P = 128
+PACK = 4
+K_PASS = P * PACK
+B, IN, HID, BLK = 512, 1024, 4096, 512
+NB = HID // BLK
+X_PASSES = IN // K_PASS
+B_TILES = B // P
+H_TILES = BLK // P
+LAG = 2
+AHEAD = 3
+
+FLOPS = 2 * B * IN * HID + 2 * B * BLK * HID
+
+
+def tile_blockdiagmnistconvertible_pa_kernel(tc, x, W1_words, W1_scales, b1, Wb, bb, out):
+    nc = tc.nc
+    with ExitStack() as ctx:
+        consts = ctx.enter_context(tc.tile_pool(name="consts", bufs=1))
+        w1_pool = ctx.enter_context(tc.tile_pool(name="w1", bufs=AHEAD + 1))
+        wb_pool = ctx.enter_context(tc.tile_pool(name="wb", bufs=AHEAD + 1))
+        work = ctx.enter_context(tc.tile_pool(name="work", bufs=2))
+        quant = ctx.enter_context(tc.tile_pool(name="quant", bufs=LAG + 2))
+        res_pool = ctx.enter_context(tc.tile_pool(name="res", bufs=4))
+        pw_pool = ctx.enter_context(tc.psum_pool(name="pw", bufs=2))
+        ph_pool = ctx.enter_context(tc.psum_pool(name="ph", bufs=3))
+        py_pool = ctx.enter_context(tc.psum_pool(name="py", bufs=3))
+        ctx.enter_context(tc.manual_schedule())
+
+        w1_planes = consts.tile([P, HID], U8, align_bytes=64)
+        nc.vector.memset(w1_planes[:].bitcast(I32), 0)
+        b1_rows = consts.tile([P, P], BF16)
+        nc.vector.memset(b1_rows[:].bitcast(I32), 0)
+        ident_f32 = consts.tile([P, P], F32)
+        make_identity(nc, ident_f32[:])
+        ident_bf = consts.tile([P, P], BF16)
+        make_identity(nc, ident_bf[:])
+        nc.scalar.dma_start(out=b1_rows[0 : HID // P, :], in_=b1.rearrange("(j p) -> j p", p=P))
+
+        x_sb = []
+        for i in range(B_TILES):
+            x_rows = consts.tile([P, IN], BF16, name="x_rows%d" % i)
+            nc.sync.dma_start(out=x_rows[:], in_=x[i * P : (i + 1) * P, :])
+            x_sb.append(x_rows)
+
+        w1_words = {}
+        wb_rows = {}
+
+        def load_weights(n):
+            wb_rows[n] = wb_pool.tile([P, H_TILES, BLK], BF16, name="wb_rows")
+            nc.sync.dma_start(out=wb_rows[n][:], in_=Wb[n].rearrange("(j p) k -> p j k", p=P))
+            w1_words[n] = w1_pool.tile([P, X_PASSES, BLK], U32, name="w1_words", align_bytes=64)
+            nc.sync.dma_start(
+                out=w1_words[n][:].bitcast(I32),
+                in_=W1_words.rearrange("g p n t -> p g (n t)")[:, :, n * BLK * PACK : (n + 1) * BLK * PACK].bitcast(I32),
+            )
+
+        for q in range(4):
+            nc.sync.dma_start(
+                out=w1_planes[32 * q : 32 * q + 4 * X_PASSES, :].bitcast(I32),
+                in_=W1_scales[:, 4 * q : 4 * q + 4, :].bitcast(I32),
+            )
+        load_weights(0)
+        load_weights(1)
+        bb_all = consts.tile([P, HID], BF16)
+        nc.sync.dma_start(out=bb_all[:], in_=bb.partition_broadcast(P))
+        load_weights(2)
+
+        pb = pw_pool.tile([P, P], BF16, tag="pw")
+        nc.tensor.transpose(pb[:], b1_rows[:], ident_bf[:])
+        b1_cols = consts.tile([P, HID // P], F32)
+        nc.vector.tensor_copy(out=b1_cols[:], in_=pb[:, 0 : HID // P])
+
+        x_grouped = consts.tile([P, X_PASSES, B, PACK], BF16, align_bytes=64)
+        x_codes = consts.tile([P, X_PASSES, B], U32, align_bytes=64)
+        x_planes = consts.tile([P, X_PASSES, B], U8, align_bytes=64)
+        for i in range(B_TILES):
+            rows = slice(i * P, (i + 1) * P)
+            px = py_pool.tile([P, X_PASSES, 2, P], F32, tag="py")
+            x_words = x_sb[i][:].bitcast(F32)
+            for g in range(X_PASSES):
+                for u in range(2):
+                    nc.tensor.transpose(px[:, g, u, :], x_words[:, 256 * g + u : 256 * (g + 1) : 2], ident_f32[:])
+            nc.scalar.copy(
+                out=x_grouped[:].bitcast(F32)[:, :, rows, :],
+                in_=px[:].rearrange("p g u b -> p g b u"),
+            )
+            for g in range(X_PASSES):
+                nc.vector.quantize_mx(
+                    out=x_codes[:, g, rows].bitcast(FP8X4),
+                    scales=x_planes[:, g, rows],
+                    in_=x_grouped[:, g, rows, :].rearrange("p b t -> p (b t)"),
+                )
+
+        wb_grouped = {}
+        wb_codes = {}
+        wb_planes = {}
+        h_plain = {}
+        h_codes = {}
+        h_planes = {}
+
+        def transpose_wb(n):
+            wb_grouped[n] = work.tile([P, BLK, PACK], BF16, name="wb_grouped", align_bytes=64)
+            for half in range(2):
+                pw = pw_pool.tile([P, PACK, 2 * P], BF16, tag="pw")
+                for jj in range(2):
+                    for t in range(PACK):
+                        nc.tensor.transpose(
+                            pw[:, t, jj * P : (jj + 1) * P],
+                            wb_rows[n][:, 2 * half + jj, t * P : (t + 1) * P],
+                            ident_bf[:],
+                        )
+                nc.scalar.copy(
+                    out=wb_grouped[n][:, half * 2 * P : (half + 1) * 2 * P, :],
+                    in_=pw[:].rearrange("p t o -> p o t"),
+                )
+
+        def quantise_wb(n):
+            wb_codes[n] = quant.tile([P, BLK], U32, name="wb_codes", align_bytes=64)
+            wb_planes[n] = quant.tile([P, BLK], U8, name="wb_planes", align_bytes=64)
+            nc.vector.quantize_mx(
+                out=wb_codes[n][:].bitcast(FP8X4),
+                scales=wb_planes[n][:],
+                in_=wb_grouped[n][:].rearrange("p o t -> p (o t)"),
+            )
+
+        def first_product(n, t):
+            cols = slice(t * P, (t + 1) * P)
+            ph = ph_pool.tile([P, B], F32, tag="ph")
+            for g in range(X_PASSES):
+                nc.tensor.matmul_mx(
+                    out=ph[:],
+                    lhsT=w1_words[n][:, g, cols].bitcast(FP8X4),
+                    lhsT_scale=w1_planes[4 * g : P, n * BLK + t * P : n * BLK + (t + 1) * P],
+                    rhs=x_codes[:, g, :].bitcast(FP8X4),
+                    rhs_scale=x_planes[:, g, :],
+                    start=(g == 0),
+                    stop=(g == X_PASSES - 1),
+                )
+            j = n * H_TILES + t
+            nc.scalar.activation(out=h_plain[n][:, t, :], in_=ph[:], func=RELU, bias=b1_cols[:, j : j + 1], scale=1.0)
+
+        def regroup_h(n):
+            h_grouped = work.tile([P, B, PACK], BF16, name="h_grouped", align_bytes=64)
+            nc.vector.tensor_copy(
+                out=h_grouped[:].rearrange("p (c i) t -> p c t i", i=4),
+                in_=h_plain[n][:].rearrange("p t (c i) -> p c t i", i=4),
+            )
+            return h_grouped
+
+        def quantise_h(n, h_grouped):
+            h_codes[n] = quant.tile([P, B], U32, name="h_codes", align_bytes=64)
+            h_planes[n] = quant.tile([P, B], U8, name="h_planes", align_bytes=64)
+            nc.vector.quantize_mx(
+                out=h_codes[n][:].bitcast(FP8X4),
+                scales=h_planes[n][:],
+                in_=h_grouped[:].rearrange("p b t -> p (b t)"),
+            )
+
+        def second_product(n, i, res):
+            rows = slice(i * P, (i + 1) * P)
+            py = py_pool.tile([P, BLK], F32, tag="py")
+            nc.tensor.matmul_mx(
+                out=py[:],
+                lhsT=h_codes[n][:, rows].bitcast(FP8X4),
+                lhsT_scale=h_planes[n][:, rows],
+                rhs=wb_codes[n][:].bitcast(FP8X4),
+                rhs_scale=wb_planes[n][:],
+                start=True,
+                stop=True,
+            )
+            nc.vector.tensor_tensor(out=res[:, i % 2, :], in0=py[:], in1=bb_all[:, n * BLK : (n + 1) * BLK], op=ADD)
+
+        out_tiles = out.rearrange("(i p) c -> p i c", p=P)
+
+        for m in range(NB + LAG):
+            if m + AHEAD < NB:
+                load_weights(m + AHEAD)
+            if m < NB:
+                transpose_wb(m)
+                h_plain[m] = work.tile([P, H_TILES, B], BF16, name="h_plain")
+            if 1 <= m <= NB:
+                h_grouped = regroup_h(m - 1)
+                quantise_wb(m - 1)
+                quantise_h(m - 1, h_grouped)
+            res = None
+            for t in range(H_TILES):
+                if m < NB:
+                    first_product(m, t)
+                if m >= LAG:
+                    n = m - LAG
+                    if t % 2 == 0:
+                        res = res_pool.tile([P, 2, BLK], F32, name="res")
+                    second_product(n, t, res)
+                    if t % 2 == 1:
+                        nc.gpsimd.tensor_scalar(out=res[:], in0=res[:], scalar1=0.0, scalar2=0.0, op0=MAX, op1=ADD)
+                        nc.sync.dma_start(out=out_tiles[:, t - 1 : t + 1, n * BLK : (n + 1) * BLK], in_=res[:])

@@ -12,6 +12,8 @@ FP8X4 = mybir.dt.float8_e4m3fn_x4
 RELU = mybir.ActivationFunctionType.Relu
 ADD = mybir.AluOpType.add
 MAX = mybir.AluOpType.max
+MIN = mybir.AluOpType.min
+FLT_MAX = 3.4028235e38
 
 P = 128
 PACK = 4
@@ -35,7 +37,7 @@ def tile_blockdiagmnistconvertible_pa_kernel(tc, x, W1_words, W1_scales, b1, Wb,
         wb_pool = ctx.enter_context(tc.tile_pool(name="wb", bufs=AHEAD + 1))
         work = ctx.enter_context(tc.tile_pool(name="work", bufs=2))
         quant = ctx.enter_context(tc.tile_pool(name="quant", bufs=LAG + 2))
-        res_pool = ctx.enter_context(tc.tile_pool(name="res", bufs=4))
+        res_pool = ctx.enter_context(tc.tile_pool(name="res", bufs=8))
         pw_pool = ctx.enter_context(tc.psum_pool(name="pw", bufs=2))
         ph_pool = ctx.enter_context(tc.psum_pool(name="ph", bufs=3))
         py_pool = ctx.enter_context(tc.psum_pool(name="py", bufs=3))
@@ -60,25 +62,30 @@ def tile_blockdiagmnistconvertible_pa_kernel(tc, x, W1_words, W1_scales, b1, Wb,
         w1_words = {}
         wb_rows = {}
 
-        def load_weights(n):
-            wb_rows[n] = wb_pool.tile([P, H_TILES, BLK], BF16, name="wb_rows")
-            nc.sync.dma_start(out=wb_rows[n][:], in_=Wb[n].rearrange("(j p) k -> p j k", p=P))
+        def load_w1(n):
             w1_words[n] = w1_pool.tile([P, X_PASSES, BLK], U32, name="w1_words", align_bytes=64)
             nc.sync.dma_start(
                 out=w1_words[n][:].bitcast(I32),
                 in_=W1_words.rearrange("g p n t -> p g (n t)")[:, :, n * BLK * PACK : (n + 1) * BLK * PACK].bitcast(I32),
             )
 
+        def load_wb(n):
+            wb_rows[n] = wb_pool.tile([P, H_TILES, BLK], BF16, name="wb_rows")
+            nc.sync.dma_start(out=wb_rows[n][:], in_=Wb[n].rearrange("(j p) k -> p j k", p=P))
+
+        load_w1(0)
         for q in range(4):
             nc.sync.dma_start(
                 out=w1_planes[32 * q : 32 * q + 4 * X_PASSES, :].bitcast(I32),
                 in_=W1_scales[:, 4 * q : 4 * q + 4, :].bitcast(I32),
             )
-        load_weights(0)
-        load_weights(1)
+        load_wb(0)
+        load_w1(1)
+        load_wb(1)
         bb_all = consts.tile([P, HID], BF16)
         nc.sync.dma_start(out=bb_all[:], in_=bb.partition_broadcast(P))
-        load_weights(2)
+        load_w1(2)
+        load_wb(2)
 
         pb = pw_pool.tile([P, P], BF16, tag="pw")
         nc.tensor.transpose(pb[:], b1_rows[:], ident_bf[:])
@@ -154,24 +161,24 @@ def tile_blockdiagmnistconvertible_pa_kernel(tc, x, W1_words, W1_scales, b1, Wb,
             j = n * H_TILES + t
             nc.scalar.activation(out=h_plain[n][:, t, :], in_=ph[:], func=RELU, bias=b1_cols[:, j : j + 1], scale=1.0)
 
-        def regroup_h(n):
+        def quantise_h(n):
             h_grouped = work.tile([P, B, PACK], BF16, name="h_grouped", align_bytes=64)
-            nc.vector.tensor_copy(
-                out=h_grouped[:].rearrange("p (c i) t -> p c t i", i=4),
-                in_=h_plain[n][:].rearrange("p t (c i) -> p c t i", i=4),
-            )
-            return h_grouped
-
-        def quantise_h(n, h_grouped):
             h_codes[n] = quant.tile([P, B], U32, name="h_codes", align_bytes=64)
             h_planes[n] = quant.tile([P, B], U8, name="h_planes", align_bytes=64)
-            nc.vector.quantize_mx(
-                out=h_codes[n][:].bitcast(FP8X4),
-                scales=h_planes[n][:],
-                in_=h_grouped[:].rearrange("p b t -> p (b t)"),
-            )
+            halves = [slice(0, B // 2), slice(B // 2, B)]
+            for cols in halves:
+                nc.vector.tensor_copy(
+                    out=h_grouped[:, cols, :].rearrange("p (c i) t -> p c t i", i=4),
+                    in_=h_plain[n][:, :, cols].rearrange("p t (c i) -> p c t i", i=4),
+                )
+            for cols in halves:
+                nc.vector.quantize_mx(
+                    out=h_codes[n][:, cols].bitcast(FP8X4),
+                    scales=h_planes[n][:, cols],
+                    in_=h_grouped[:, cols, :].rearrange("p b t -> p (b t)"),
+                )
 
-        def second_product(n, i, res):
+        def second_product(n, i):
             rows = slice(i * P, (i + 1) * P)
             py = py_pool.tile([P, BLK], F32, tag="py")
             nc.tensor.matmul_mx(
@@ -183,29 +190,23 @@ def tile_blockdiagmnistconvertible_pa_kernel(tc, x, W1_words, W1_scales, b1, Wb,
                 start=True,
                 stop=True,
             )
-            nc.vector.tensor_tensor(out=res[:, i % 2, :], in0=py[:], in1=bb_all[:, n * BLK : (n + 1) * BLK], op=ADD)
-
-        out_tiles = out.rearrange("(i p) c -> p i c", p=P)
+            res = res_pool.tile([P, BLK], F32, name="res")
+            nc.vector.tensor_tensor(out=res[:], in0=py[:], in1=bb_all[:, n * BLK : (n + 1) * BLK], op=ADD)
+            nc.gpsimd.tensor_scalar(out=res[:], in0=res[:], scalar1=FLT_MAX, scalar2=0.0, op0=MIN, op1=MAX)
+            nc.sync.dma_start(out=out[rows, n * BLK : (n + 1) * BLK], in_=res[:])
 
         for m in range(NB + LAG):
             if m + AHEAD < NB:
-                load_weights(m + AHEAD)
+                load_w1(m + AHEAD)
+                load_wb(m + AHEAD)
             if m < NB:
-                transpose_wb(m)
                 h_plain[m] = work.tile([P, H_TILES, B], BF16, name="h_plain")
-            if 1 <= m <= NB:
-                h_grouped = regroup_h(m - 1)
-                quantise_wb(m - 1)
-                quantise_h(m - 1, h_grouped)
-            res = None
             for t in range(H_TILES):
                 if m < NB:
                     first_product(m, t)
                 if m >= LAG:
-                    n = m - LAG
-                    if t % 2 == 0:
-                        res = res_pool.tile([P, 2, BLK], F32, name="res")
-                    second_product(n, t, res)
-                    if t % 2 == 1:
-                        nc.gpsimd.tensor_scalar(out=res[:], in0=res[:], scalar1=0.0, scalar2=0.0, op0=MAX, op1=ADD)
-                        nc.sync.dma_start(out=out_tiles[:, t - 1 : t + 1, n * BLK : (n + 1) * BLK], in_=res[:])
+                    second_product(m - LAG, t)
+            if m < NB:
+                transpose_wb(m)
+                quantise_h(m)
+                quantise_wb(m)

@@ -12,8 +12,6 @@ FP8X4 = mybir.dt.float8_e4m3fn_x4
 RELU = mybir.ActivationFunctionType.Relu
 ADD = mybir.AluOpType.add
 MAX = mybir.AluOpType.max
-MIN = mybir.AluOpType.min
-FLT_MAX = 3.4028235e38
 
 P = 128
 PACK = 4
@@ -192,9 +190,16 @@ def tile_blockdiagmnistconvertible_pa_kernel(tc, x, W1_words, W1_scales, b1, Wb,
             )
             res = res_pool.tile([P, BLK], F32, name="res")
             nc.vector.tensor_tensor(out=res[:], in0=py[:], in1=bb_all[:, n * BLK : (n + 1) * BLK], op=ADD)
-            nc.gpsimd.tensor_scalar(out=res[:], in0=res[:], scalar1=FLT_MAX, scalar2=0.0, op0=MIN, op1=MAX)
-            nc.sync.dma_start(out=out[rows, n * BLK : (n + 1) * BLK], in_=res[:])
+            return res
 
+        def relu_and_store(n, i, res):
+            if i % 2 == 0:
+                nc.vector.tensor_scalar_max(out=res[:], in0=res[:], scalar1=0.0)
+            else:
+                nc.scalar.activation(out=res[:], in_=res[:], func=RELU)
+            nc.sync.dma_start(out=out[i * P : (i + 1) * P, n * BLK : (n + 1) * BLK], in_=res[:])
+
+        waiting = []
         for m in range(NB + LAG):
             if m + AHEAD < NB:
                 load_w1(m + AHEAD)
@@ -205,8 +210,11 @@ def tile_blockdiagmnistconvertible_pa_kernel(tc, x, W1_words, W1_scales, b1, Wb,
                 if m < NB:
                     first_product(m, t)
                 if m >= LAG:
-                    second_product(m - LAG, t)
+                    waiting.append((m - LAG, t, second_product(m - LAG, t)))
+                if len(waiting) == 2:
+                    relu_and_store(*waiting.pop(0))
             if m < NB:
                 transpose_wb(m)
                 quantise_h(m)
                 quantise_wb(m)
+        relu_and_store(*waiting.pop(0))

@@ -12,6 +12,8 @@ FP8X4 = mybir.dt.float8_e4m3fn_x4
 RELU = mybir.ActivationFunctionType.Relu
 ADD = mybir.AluOpType.add
 MAX = mybir.AluOpType.max
+MIN = mybir.AluOpType.min
+FLT_MAX = 3.4028235e38
 
 P = 128
 PACK = 4
@@ -41,10 +43,10 @@ def tile_blockdiagmnistconvertible_pa_kernel(tc, x, W1_words, W1_scales, b1, Wb,
         py_pool = ctx.enter_context(tc.psum_pool(name="py", bufs=3))
         ctx.enter_context(tc.manual_schedule())
 
-        w1_planes = consts.tile([P, HID], U8, align_bytes=64)
-        nc.vector.memset(w1_planes[:].bitcast(I32), 0)
         b1_rows = consts.tile([P, P], BF16)
         nc.vector.memset(b1_rows[:].bitcast(I32), 0)
+        w1_planes = consts.tile([P, HID], U8, align_bytes=64)
+        nc.vector.memset(w1_planes[:].bitcast(I32), 0)
         ident_f32 = consts.tile([P, P], F32)
         make_identity(nc, ident_f32[:])
         ident_bf = consts.tile([P, P], BF16)
@@ -59,6 +61,7 @@ def tile_blockdiagmnistconvertible_pa_kernel(tc, x, W1_words, W1_scales, b1, Wb,
 
         w1_words = {}
         wb_rows = {}
+        bb_rows = {}
 
         def load_w1(n):
             w1_words[n] = w1_pool.tile([P, X_PASSES, BLK], U32, name="w1_words", align_bytes=64)
@@ -68,8 +71,11 @@ def tile_blockdiagmnistconvertible_pa_kernel(tc, x, W1_words, W1_scales, b1, Wb,
             )
 
         def load_wb(n):
-            wb_rows[n] = wb_pool.tile([P, H_TILES, BLK], BF16, name="wb_rows")
-            nc.sync.dma_start(out=wb_rows[n][:], in_=Wb[n].rearrange("(j p) k -> p j k", p=P))
+            wb_rows[n] = wb_pool.tile([P, 2 * BLK // P, BLK // 2], BF16, name="wb_rows")
+            half_rows = Wb[n].rearrange("o (u c) -> (o u) c", u=2)
+            nc.sync.dma_start(out=wb_rows[n][:], in_=half_rows.rearrange("(a q) c -> q a c", q=P))
+            bb_rows[n] = consts.tile([P, BLK], BF16, name="bb_rows%d" % n)
+            nc.sync.dma_start(out=bb_rows[n][:], in_=bb[n * BLK : (n + 1) * BLK].partition_broadcast(P))
 
         load_w1(0)
         for q in range(4):
@@ -80,15 +86,8 @@ def tile_blockdiagmnistconvertible_pa_kernel(tc, x, W1_words, W1_scales, b1, Wb,
         load_wb(0)
         load_w1(1)
         load_wb(1)
-        bb_all = consts.tile([P, HID], BF16)
-        nc.sync.dma_start(out=bb_all[:], in_=bb.partition_broadcast(P))
         load_w1(2)
         load_wb(2)
-
-        pb = pw_pool.tile([P, P], BF16, tag="pw")
-        nc.tensor.transpose(pb[:], b1_rows[:], ident_bf[:])
-        b1_cols = consts.tile([P, HID // P], F32)
-        nc.vector.tensor_copy(out=b1_cols[:], in_=pb[:, 0 : HID // P])
 
         x_grouped = consts.tile([P, X_PASSES, B, PACK], BF16, align_bytes=64)
         x_codes = consts.tile([P, X_PASSES, B], U32, align_bytes=64)
@@ -111,6 +110,11 @@ def tile_blockdiagmnistconvertible_pa_kernel(tc, x, W1_words, W1_scales, b1, Wb,
                     in_=x_grouped[:, g, rows, :].rearrange("p b t -> p (b t)"),
                 )
 
+        pb = pw_pool.tile([P, P], BF16, tag="pw")
+        nc.tensor.transpose(pb[:], b1_rows[:], ident_bf[:])
+        b1_cols = consts.tile([P, HID // P], F32)
+        nc.vector.tensor_copy(out=b1_cols[:], in_=pb[:, 0 : HID // P])
+
         wb_grouped = {}
         wb_codes = {}
         wb_planes = {}
@@ -121,17 +125,13 @@ def tile_blockdiagmnistconvertible_pa_kernel(tc, x, W1_words, W1_scales, b1, Wb,
         def transpose_wb(n):
             wb_grouped[n] = work.tile([P, BLK, PACK], BF16, name="wb_grouped", align_bytes=64)
             for half in range(2):
-                pw = pw_pool.tile([P, PACK, 2 * P], BF16, tag="pw")
-                for jj in range(2):
-                    for t in range(PACK):
-                        nc.tensor.transpose(
-                            pw[:, t, jj * P : (jj + 1) * P],
-                            wb_rows[n][:, 2 * half + jj, t * P : (t + 1) * P],
-                            ident_bf[:],
-                        )
+                pw = pw_pool.tile([P, 2, 4, P], BF16, tag="pw")
+                for a in range(4):
+                    for c in range(2):
+                        nc.tensor.transpose(pw[:, c, a, :], wb_rows[n][:, 4 * half + a, c * P : (c + 1) * P], ident_bf[:])
                 nc.scalar.copy(
-                    out=wb_grouped[n][:, half * 2 * P : (half + 1) * 2 * P, :],
-                    in_=pw[:].rearrange("p t o -> p o t"),
+                    out=wb_grouped[n][:].bitcast(F32)[:, half * 2 * P : (half + 1) * 2 * P, :],
+                    in_=pw[:].bitcast(F32).rearrange("p c a w -> p (a w) c"),
                 )
 
         def quantise_wb(n):
@@ -157,7 +157,8 @@ def tile_blockdiagmnistconvertible_pa_kernel(tc, x, W1_words, W1_scales, b1, Wb,
                     stop=(g == X_PASSES - 1),
                 )
             j = n * H_TILES + t
-            nc.scalar.activation(out=h_plain[n][:, t, :], in_=ph[:], func=RELU, bias=b1_cols[:, j : j + 1], scale=1.0)
+            place = 2 * (t % 2) + t // 2
+            nc.scalar.activation(out=h_plain[n][:, place, :], in_=ph[:], func=RELU, bias=b1_cols[:, j : j + 1], scale=1.0)
 
         def quantise_h(n):
             h_grouped = work.tile([P, B, PACK], BF16, name="h_grouped", align_bytes=64)
@@ -189,12 +190,12 @@ def tile_blockdiagmnistconvertible_pa_kernel(tc, x, W1_words, W1_scales, b1, Wb,
                 stop=True,
             )
             res = res_pool.tile([P, BLK], F32, name="res")
-            nc.vector.tensor_tensor(out=res[:], in0=py[:], in1=bb_all[:, n * BLK : (n + 1) * BLK], op=ADD)
+            nc.vector.tensor_tensor(out=res[:], in0=py[:], in1=bb_rows[n][:], op=ADD)
             return res
 
         def relu_and_store(n, i, res):
             if i % 2 == 0:
-                nc.vector.tensor_scalar_max(out=res[:], in0=res[:], scalar1=0.0)
+                nc.gpsimd.tensor_scalar(out=res[:], in0=res[:], scalar1=FLT_MAX, scalar2=0.0, op0=MIN, op1=MAX)
             else:
                 nc.scalar.activation(out=res[:], in_=res[:], func=RELU)
             nc.sync.dma_start(out=out[i * P : (i + 1) * P, n * BLK : (n + 1) * BLK], in_=res[:])

@@ -23,7 +23,8 @@ NB = HID // BLK
 X_PASSES = IN // K_PASS
 B_TILES = B // P
 H_TILES = BLK // P
-LAG = 2
+HALF = B // 2
+LAG = 7
 AHEAD = 3
 
 FLOPS = 2 * B * IN * HID + 2 * B * BLK * HID
@@ -36,7 +37,7 @@ def tile_blockdiagmnistconvertible_pa_kernel(tc, x, W1_words, W1_scales, b1, Wb,
         w1_pool = ctx.enter_context(tc.tile_pool(name="w1", bufs=AHEAD + 1))
         wb_pool = ctx.enter_context(tc.tile_pool(name="wb", bufs=AHEAD + 1))
         work = ctx.enter_context(tc.tile_pool(name="work", bufs=2))
-        quant = ctx.enter_context(tc.tile_pool(name="quant", bufs=LAG + 2))
+        quant = ctx.enter_context(tc.tile_pool(name="quant", bufs=4))
         res_pool = ctx.enter_context(tc.tile_pool(name="res", bufs=8))
         pw_pool = ctx.enter_context(tc.psum_pool(name="pw", bufs=2))
         ph_pool = ctx.enter_context(tc.psum_pool(name="ph", bufs=3))
@@ -89,7 +90,6 @@ def tile_blockdiagmnistconvertible_pa_kernel(tc, x, W1_words, W1_scales, b1, Wb,
         load_w1(2)
         load_wb(2)
 
-        x_grouped = consts.tile([P, X_PASSES, B, PACK], BF16, align_bytes=64)
         x_codes = consts.tile([P, X_PASSES, B], U32, align_bytes=64)
         x_planes = consts.tile([P, X_PASSES, B], U8, align_bytes=64)
         for i in range(B_TILES):
@@ -99,23 +99,23 @@ def tile_blockdiagmnistconvertible_pa_kernel(tc, x, W1_words, W1_scales, b1, Wb,
             for g in range(X_PASSES):
                 for u in range(2):
                     nc.tensor.transpose(px[:, g, u, :], x_words[:, 256 * g + u : 256 * (g + 1) : 2], ident_f32[:])
-            nc.scalar.copy(
-                out=x_grouped[:].bitcast(F32)[:, :, rows, :],
-                in_=px[:].rearrange("p g u b -> p g b u"),
-            )
+            x_grouped = consts.tile([P, X_PASSES, P, PACK], BF16, name="x_grouped%d" % i, align_bytes=64)
+            nc.scalar.copy(out=x_grouped[:].bitcast(F32), in_=px[:].rearrange("p g u b -> p g b u"))
+            if i == B_TILES - 1:
+                pb = pw_pool.tile([P, P], BF16, tag="pw")
+                nc.tensor.transpose(pb[:], b1_rows[:], ident_bf[:])
+                b1_cols = consts.tile([P, HID // P], F32)
+                nc.vector.tensor_copy(out=b1_cols[:], in_=pb[:, 0 : HID // P])
             for g in range(X_PASSES):
                 nc.vector.quantize_mx(
                     out=x_codes[:, g, rows].bitcast(FP8X4),
                     scales=x_planes[:, g, rows],
-                    in_=x_grouped[:, g, rows, :].rearrange("p b t -> p (b t)"),
+                    in_=x_grouped[:, g, :, :].rearrange("p b t -> p (b t)"),
                 )
 
-        pb = pw_pool.tile([P, P], BF16, tag="pw")
-        nc.tensor.transpose(pb[:], b1_rows[:], ident_bf[:])
-        b1_cols = consts.tile([P, HID // P], F32)
-        nc.vector.tensor_copy(out=b1_cols[:], in_=pb[:, 0 : HID // P])
-
+        wb_banks = {}
         wb_grouped = {}
+        h_grouped = {}
         wb_codes = {}
         wb_planes = {}
         h_plain = {}
@@ -129,10 +129,13 @@ def tile_blockdiagmnistconvertible_pa_kernel(tc, x, W1_words, W1_scales, b1, Wb,
                 for a in range(4):
                     for c in range(2):
                         nc.tensor.transpose(pw[:, c, a, :], wb_rows[n][:, 4 * half + a, c * P : (c + 1) * P], ident_bf[:])
-                nc.scalar.copy(
-                    out=wb_grouped[n][:].bitcast(F32)[:, half * 2 * P : (half + 1) * 2 * P, :],
-                    in_=pw[:].bitcast(F32).rearrange("p c a w -> p (a w) c"),
-                )
+                wb_banks[n, half] = pw
+
+        def copy_wb(n, half):
+            nc.scalar.copy(
+                out=wb_grouped[n][:].bitcast(F32)[:, half * 2 * P : (half + 1) * 2 * P, :],
+                in_=wb_banks[n, half][:].bitcast(F32).rearrange("p c a w -> p (a w) c"),
+            )
 
         def quantise_wb(n):
             wb_codes[n] = quant.tile([P, BLK], U32, name="wb_codes", align_bytes=64)
@@ -143,39 +146,45 @@ def tile_blockdiagmnistconvertible_pa_kernel(tc, x, W1_words, W1_scales, b1, Wb,
                 in_=wb_grouped[n][:].rearrange("p o t -> p (o t)"),
             )
 
-        def first_product(n, t):
-            cols = slice(t * P, (t + 1) * P)
+        def first_product(n, t, cols):
+            hidden = slice(t * P, (t + 1) * P)
             ph = ph_pool.tile([P, B], F32, tag="ph")
+            width = cols.stop - cols.start
             for g in range(X_PASSES):
                 nc.tensor.matmul_mx(
-                    out=ph[:],
-                    lhsT=w1_words[n][:, g, cols].bitcast(FP8X4),
+                    out=ph[:, 0:width],
+                    lhsT=w1_words[n][:, g, hidden].bitcast(FP8X4),
                     lhsT_scale=w1_planes[4 * g : P, n * BLK + t * P : n * BLK + (t + 1) * P],
-                    rhs=x_codes[:, g, :].bitcast(FP8X4),
-                    rhs_scale=x_planes[:, g, :],
+                    rhs=x_codes[:, g, cols].bitcast(FP8X4),
+                    rhs_scale=x_planes[:, g, cols],
                     start=(g == 0),
                     stop=(g == X_PASSES - 1),
                 )
             j = n * H_TILES + t
             place = 2 * (t % 2) + t // 2
-            nc.scalar.activation(out=h_plain[n][:, place, :], in_=ph[:], func=RELU, bias=b1_cols[:, j : j + 1], scale=1.0)
+            nc.scalar.activation(out=h_plain[n][:, place, cols], in_=ph[:, 0:width], func=RELU, bias=b1_cols[:, j : j + 1], scale=1.0)
 
-        def quantise_h(n):
-            h_grouped = work.tile([P, B, PACK], BF16, name="h_grouped", align_bytes=64)
-            h_codes[n] = quant.tile([P, B], U32, name="h_codes", align_bytes=64)
-            h_planes[n] = quant.tile([P, B], U8, name="h_planes", align_bytes=64)
-            halves = [slice(0, B // 2), slice(B // 2, B)]
-            for cols in halves:
-                nc.vector.tensor_copy(
-                    out=h_grouped[:, cols, :].rearrange("p (c i) t -> p c t i", i=4),
-                    in_=h_plain[n][:, :, cols].rearrange("p t (c i) -> p c t i", i=4),
-                )
-            for cols in halves:
-                nc.vector.quantize_mx(
-                    out=h_codes[n][:, cols].bitcast(FP8X4),
-                    scales=h_planes[n][:, cols],
-                    in_=h_grouped[:, cols, :].rearrange("p b t -> p (b t)"),
-                )
+        halves = [slice(0, HALF), slice(HALF, B)]
+
+        def regroup_h(n, half):
+            if half == 0:
+                h_grouped[n] = work.tile([P, B, PACK], BF16, name="h_grouped", align_bytes=64)
+            cols = halves[half]
+            nc.vector.tensor_copy(
+                out=h_grouped[n][:, cols, :].rearrange("p (c i) t -> p c t i", i=4),
+                in_=h_plain[n][:, :, cols].rearrange("p t (c i) -> p c t i", i=4),
+            )
+
+        def quantise_h(n, half):
+            if half == 0:
+                h_codes[n] = quant.tile([P, B], U32, name="h_codes", align_bytes=64)
+                h_planes[n] = quant.tile([P, B], U8, name="h_planes", align_bytes=64)
+            cols = halves[half]
+            nc.vector.quantize_mx(
+                out=h_codes[n][:, cols].bitcast(FP8X4),
+                scales=h_planes[n][:, cols],
+                in_=h_grouped[n][:, cols, :].rearrange("p b t -> p (b t)"),
+            )
 
         def second_product(n, i):
             rows = slice(i * P, (i + 1) * P)
@@ -201,21 +210,40 @@ def tile_blockdiagmnistconvertible_pa_kernel(tc, x, W1_words, W1_scales, b1, Wb,
             nc.sync.dma_start(out=out[i * P : (i + 1) * P, n * BLK : (n + 1) * BLK], in_=res[:])
 
         waiting = []
-        for m in range(NB + LAG):
-            if m + AHEAD < NB:
-                load_w1(m + AHEAD)
-                load_wb(m + AHEAD)
-            if m < NB:
-                h_plain[m] = work.tile([P, H_TILES, B], BF16, name="h_plain")
-            for t in range(H_TILES):
-                if m < NB:
-                    first_product(m, t)
-                if m >= LAG:
-                    waiting.append((m - LAG, t, second_product(m - LAG, t)))
-                if len(waiting) == 2:
-                    relu_and_store(*waiting.pop(0))
-            if m < NB:
-                transpose_wb(m)
-                quantise_h(m)
-                quantise_wb(m)
-        relu_and_store(*waiting.pop(0))
+        for step in range(NB * H_TILES + LAG):
+            n, t = divmod(step, H_TILES)
+            if t == 0 and n + AHEAD < NB:
+                load_w1(n + AHEAD)
+                load_wb(n + AHEAD)
+            if t == 0 and n < NB:
+                h_plain[n] = work.tile([P, H_TILES, B], BF16, name="h_plain")
+            if step == 0:
+                for half in range(2):
+                    for first in range(H_TILES):
+                        first_product(0, first, halves[half])
+                    if half == 0:
+                        regroup_h(0, 0)
+                quantise_h(0, 0)
+            elif H_TILES <= step < NB * H_TILES:
+                first_product(n, t, slice(0, B))
+            if t == 0 and 1 <= n <= NB:
+                if n > 1:
+                    regroup_h(n - 1, 0)
+                regroup_h(n - 1, 1)
+            if t == 1 and 1 <= n <= NB:
+                quantise_wb(n - 1)
+            if step >= LAG:
+                m, i = divmod(step - LAG, B_TILES)
+                waiting.append((m, i, second_product(m, i)))
+            if t == 0 and 1 <= n <= NB:
+                if n > 1:
+                    quantise_h(n - 1, 0)
+                quantise_h(n - 1, 1)
+            if len(waiting) == 3:
+                relu_and_store(*waiting.pop(0))
+            if t == H_TILES - 1 and n < NB:
+                transpose_wb(n)
+                copy_wb(n, 0)
+                copy_wb(n, 1)
+        for last in waiting:
+            relu_and_store(*last)

@@ -44,15 +44,16 @@ def tile_blockdiagmnistconvertible_pa_kernel(tc, x, W1_words, W1_scales, b1, Wb,
         py_pool = ctx.enter_context(tc.psum_pool(name="py", bufs=3))
         ctx.enter_context(tc.manual_schedule())
 
-        b1_rows = consts.tile([P, P], BF16)
-        nc.vector.memset(b1_rows[:].bitcast(I32), 0)
+        bias_rows = consts.tile([P, P], BF16)
+        nc.vector.memset(bias_rows[:].bitcast(I32), 0)
         w1_planes = consts.tile([P, HID], U8, align_bytes=64)
         nc.vector.memset(w1_planes[:].bitcast(I32), 0)
         ident_f32 = consts.tile([P, P], F32)
         make_identity(nc, ident_f32[:])
         ident_bf = consts.tile([P, P], BF16)
         make_identity(nc, ident_bf[:])
-        nc.scalar.dma_start(out=b1_rows[0 : HID // P, :], in_=b1.rearrange("(j p) -> j p", p=P))
+        nc.scalar.dma_start(out=bias_rows[0 : HID // P, :], in_=b1.rearrange("(j p) -> j p", p=P))
+        nc.scalar.dma_start(out=bias_rows[HID // P : 2 * HID // P, :], in_=bb.rearrange("(j p) -> j p", p=P))
 
         x_sb = []
         for i in range(B_TILES):
@@ -62,7 +63,6 @@ def tile_blockdiagmnistconvertible_pa_kernel(tc, x, W1_words, W1_scales, b1, Wb,
 
         w1_words = {}
         wb_rows = {}
-        bb_rows = {}
 
         def load_w1(n):
             w1_words[n] = w1_pool.tile([P, X_PASSES, BLK], U32, name="w1_words", align_bytes=64)
@@ -75,8 +75,6 @@ def tile_blockdiagmnistconvertible_pa_kernel(tc, x, W1_words, W1_scales, b1, Wb,
             wb_rows[n] = wb_pool.tile([P, 2 * BLK // P, BLK // 2], BF16, name="wb_rows")
             half_rows = Wb[n].rearrange("o (u c) -> (o u) c", u=2)
             nc.sync.dma_start(out=wb_rows[n][:], in_=half_rows.rearrange("(a q) c -> q a c", q=P))
-            bb_rows[n] = consts.tile([P, BLK], BF16, name="bb_rows%d" % n)
-            nc.sync.dma_start(out=bb_rows[n][:], in_=bb[n * BLK : (n + 1) * BLK].partition_broadcast(P))
 
         load_w1(0)
         for q in range(4):
@@ -103,7 +101,7 @@ def tile_blockdiagmnistconvertible_pa_kernel(tc, x, W1_words, W1_scales, b1, Wb,
             nc.scalar.copy(out=x_grouped[:].bitcast(F32), in_=px[:].rearrange("p g u b -> p g b u"))
             if i == B_TILES - 1:
                 pb = pw_pool.tile([P, P], BF16, tag="pw")
-                nc.tensor.transpose(pb[:], b1_rows[:], ident_bf[:])
+                nc.tensor.transpose(pb[:], bias_rows[:], ident_bf[:])
                 b1_cols = consts.tile([P, HID // P], F32)
                 nc.vector.tensor_copy(out=b1_cols[:], in_=pb[:, 0 : HID // P])
             for g in range(X_PASSES):
@@ -113,6 +111,20 @@ def tile_blockdiagmnistconvertible_pa_kernel(tc, x, W1_words, W1_scales, b1, Wb,
                     in_=x_grouped[:, g, :, :].rearrange("p b t -> p (b t)"),
                 )
 
+        bb_spread = {}
+
+        def spread_bb(n):
+            pb = pw_pool.tile([P, 2, 4, P], BF16, tag="pw")
+            for c in range(2):
+                for j in range(4):
+                    row = HID // P + (n + c) * BLK // P + j
+                    nc.tensor.matmul(pb[:, c, j, :], lhsT=ident_bf[:, row : row + 1].to_broadcast([P, P]), rhs=bias_rows[:], start=True, stop=True)
+            pair = consts.tile([P, 2, BLK], BF16, name="bb_spread%d" % n)
+            nc.scalar.copy(out=pair[:].rearrange("p c o -> p (c o)"), in_=pb[:].rearrange("p c j o -> p (c j o)"))
+            for c in range(2):
+                bb_spread[n + c] = pair[:, c, :]
+
+        spread_bb(0)
         wb_banks = {}
         wb_grouped = {}
         h_grouped = {}
@@ -199,7 +211,7 @@ def tile_blockdiagmnistconvertible_pa_kernel(tc, x, W1_words, W1_scales, b1, Wb,
                 stop=True,
             )
             res = res_pool.tile([P, BLK], F32, name="res")
-            nc.vector.tensor_tensor(out=res[:], in0=py[:], in1=bb_rows[n][:], op=ADD)
+            nc.vector.tensor_tensor(out=res[:], in0=py[:], in1=bb_spread[n], op=ADD)
             return res
 
         def relu_and_store(n, i, res):
@@ -239,6 +251,8 @@ def tile_blockdiagmnistconvertible_pa_kernel(tc, x, W1_words, W1_scales, b1, Wb,
                 if n > 1:
                     quantise_h(n - 1, 0)
                 quantise_h(n - 1, 1)
+            if t == 2 and n % 2 == 0 and 0 < n < NB:
+                spread_bb(n)
             if len(waiting) == 3:
                 relu_and_store(*waiting.pop(0))
             if t == H_TILES - 1 and n < NB:

@@ -25,7 +25,6 @@ B_TILES = B // P
 H_TILES = BLK // P
 HALF = B // 2
 LAG = 7
-AHEAD = 3
 
 FLOPS = 2 * B * IN * HID + 2 * B * BLK * HID
 
@@ -34,11 +33,11 @@ def tile_blockdiagmnistconvertible_pa_kernel(tc, x, W1_words, W1_scales, b1, Wb,
     nc = tc.nc
     with ExitStack() as ctx:
         consts = ctx.enter_context(tc.tile_pool(name="consts", bufs=1))
-        w1_pool = ctx.enter_context(tc.tile_pool(name="w1", bufs=AHEAD + 1))
-        wb_pool = ctx.enter_context(tc.tile_pool(name="wb", bufs=AHEAD + 1))
+        w1_pool = ctx.enter_context(tc.tile_pool(name="w1", bufs=NB))
+        wb_pool = ctx.enter_context(tc.tile_pool(name="wb", bufs=NB))
         work = ctx.enter_context(tc.tile_pool(name="work", bufs=2))
         quant = ctx.enter_context(tc.tile_pool(name="quant", bufs=4))
-        res_pool = ctx.enter_context(tc.tile_pool(name="res", bufs=8))
+        res_pool = ctx.enter_context(tc.tile_pool(name="res", bufs=16))
         pw_pool = ctx.enter_context(tc.psum_pool(name="pw", bufs=2))
         ph_pool = ctx.enter_context(tc.psum_pool(name="ph", bufs=3))
         py_pool = ctx.enter_context(tc.psum_pool(name="py", bufs=3))
@@ -83,10 +82,9 @@ def tile_blockdiagmnistconvertible_pa_kernel(tc, x, W1_words, W1_scales, b1, Wb,
                 in_=W1_scales[:, 4 * q : 4 * q + 4, :].bitcast(I32),
             )
         load_wb(0)
-        load_w1(1)
-        load_wb(1)
-        load_w1(2)
-        load_wb(2)
+        for n in range(1, NB):
+            load_w1(n)
+            load_wb(n)
 
         x_codes = consts.tile([P, X_PASSES, B], U32, align_bytes=64)
         x_planes = consts.tile([P, X_PASSES, B], U8, align_bytes=64)
@@ -224,9 +222,6 @@ def tile_blockdiagmnistconvertible_pa_kernel(tc, x, W1_words, W1_scales, b1, Wb,
         waiting = []
         for step in range(NB * H_TILES + LAG):
             n, t = divmod(step, H_TILES)
-            if t == 0 and n + AHEAD < NB:
-                load_w1(n + AHEAD)
-                load_wb(n + AHEAD)
             if t == 0 and n < NB:
                 h_plain[n] = work.tile([P, H_TILES, B], BF16, name="h_plain")
             if step == 0:

@@ -124,16 +124,14 @@ def tile_blockdiagmnistconvertible_pa_kernel(tc, x, W1_words, W1_scales, b1, Wb,
 
         spread_bb(0)
         wb_banks = {}
-        wb_grouped = {}
-        h_grouped = {}
-        wb_codes = {}
-        wb_planes = {}
+        grouped = {}
         h_plain = {}
-        h_codes = {}
-        h_planes = {}
+        codes = {}
+        planes = {}
 
         def transpose_wb(n):
-            wb_grouped[n] = work.tile([P, BLK, PACK], BF16, name="wb_grouped", align_bytes=64)
+            if n > 0:
+                grouped[n] = work.tile([P, 2, BLK, PACK], BF16, name="grouped", align_bytes=64)
             for half in range(2):
                 pw = pw_pool.tile([P, 2, 4, P], BF16, tag="pw")
                 for a in range(4):
@@ -143,17 +141,8 @@ def tile_blockdiagmnistconvertible_pa_kernel(tc, x, W1_words, W1_scales, b1, Wb,
 
         def copy_wb(n, half):
             nc.scalar.copy(
-                out=wb_grouped[n][:].bitcast(F32)[:, half * 2 * P : (half + 1) * 2 * P, :],
+                out=grouped[n][:, 1, half * 2 * P : (half + 1) * 2 * P, :].bitcast(F32),
                 in_=wb_banks[n, half][:].bitcast(F32).rearrange("p c a w -> p (a w) c"),
-            )
-
-        def quantise_wb(n):
-            wb_codes[n] = quant.tile([P, BLK], U32, name="wb_codes", align_bytes=64)
-            wb_planes[n] = quant.tile([P, BLK], U8, name="wb_planes", align_bytes=64)
-            nc.vector.quantize_mx(
-                out=wb_codes[n][:].bitcast(FP8X4),
-                scales=wb_planes[n][:],
-                in_=wb_grouped[n][:].rearrange("p o t -> p (o t)"),
             )
 
         def first_product(n, t, cols):
@@ -176,24 +165,19 @@ def tile_blockdiagmnistconvertible_pa_kernel(tc, x, W1_words, W1_scales, b1, Wb,
 
         halves = [slice(0, HALF), slice(HALF, B)]
 
-        def regroup_h(n, half):
-            if half == 0:
-                h_grouped[n] = work.tile([P, B, PACK], BF16, name="h_grouped", align_bytes=64)
-            cols = halves[half]
+        def regroup_h(n, cols):
             nc.vector.tensor_copy(
-                out=h_grouped[n][:, cols, :].rearrange("p (c i) t -> p c t i", i=4),
+                out=grouped[n][:, 0, cols, :].rearrange("p (c i) t -> p c t i", i=4),
                 in_=h_plain[n][:, :, cols].rearrange("p t (c i) -> p c t i", i=4),
             )
 
-        def quantise_h(n, half):
-            if half == 0:
-                h_codes[n] = quant.tile([P, B], U32, name="h_codes", align_bytes=64)
-                h_planes[n] = quant.tile([P, B], U8, name="h_planes", align_bytes=64)
-            cols = halves[half]
+        def quantise(n):
+            codes[n] = quant.tile([P, 2, BLK], U32, name="codes", align_bytes=64)
+            planes[n] = quant.tile([P, 2, BLK], U8, name="planes", align_bytes=64)
             nc.vector.quantize_mx(
-                out=h_codes[n][:, cols].bitcast(FP8X4),
-                scales=h_planes[n][:, cols],
-                in_=h_grouped[n][:, cols, :].rearrange("p b t -> p (b t)"),
+                out=codes[n][:].rearrange("p s o -> p (s o)").bitcast(FP8X4),
+                scales=planes[n][:].rearrange("p s o -> p (s o)"),
+                in_=grouped[n][:].rearrange("p s o t -> p (s o t)"),
             )
 
         def second_product(n, i):
@@ -201,10 +185,10 @@ def tile_blockdiagmnistconvertible_pa_kernel(tc, x, W1_words, W1_scales, b1, Wb,
             py = py_pool.tile([P, BLK], F32, tag="py")
             nc.tensor.matmul_mx(
                 out=py[:],
-                lhsT=h_codes[n][:, rows].bitcast(FP8X4),
-                lhsT_scale=h_planes[n][:, rows],
-                rhs=wb_codes[n][:].bitcast(FP8X4),
-                rhs_scale=wb_planes[n][:],
+                lhsT=codes[n][:, 0, rows].bitcast(FP8X4),
+                lhsT_scale=planes[n][:, 0, rows],
+                rhs=codes[n][:, 1, :].bitcast(FP8X4),
+                rhs_scale=planes[n][:, 1, :],
                 start=True,
                 stop=True,
             )
@@ -213,7 +197,7 @@ def tile_blockdiagmnistconvertible_pa_kernel(tc, x, W1_words, W1_scales, b1, Wb,
             return res
 
         def relu_and_store(n, i, res):
-            if i % 2 == 0:
+            if i >= 2:
                 nc.gpsimd.tensor_scalar(out=res[:], in0=res[:], scalar1=FLT_MAX, scalar2=0.0, op0=MIN, op1=MAX)
             else:
                 nc.scalar.activation(out=res[:], in_=res[:], func=RELU)
@@ -229,23 +213,17 @@ def tile_blockdiagmnistconvertible_pa_kernel(tc, x, W1_words, W1_scales, b1, Wb,
                     for first in range(H_TILES):
                         first_product(0, first, halves[half])
                     if half == 0:
-                        regroup_h(0, 0)
-                quantise_h(0, 0)
+                        grouped[0] = work.tile([P, 2, BLK, PACK], BF16, name="grouped", align_bytes=64)
+                        regroup_h(0, halves[0])
             elif H_TILES <= step < NB * H_TILES:
                 first_product(n, t, slice(0, B))
             if t == 0 and 1 <= n <= NB:
-                if n > 1:
-                    regroup_h(n - 1, 0)
-                regroup_h(n - 1, 1)
-            if t == 1 and 1 <= n <= NB:
-                quantise_wb(n - 1)
+                regroup_h(n - 1, halves[1] if n == 1 else slice(0, B))
             if step >= LAG:
                 m, i = divmod(step - LAG, B_TILES)
                 waiting.append((m, i, second_product(m, i)))
             if t == 0 and 1 <= n <= NB:
-                if n > 1:
-                    quantise_h(n - 1, 0)
-                quantise_h(n - 1, 1)
+                quantise(n - 1)
             if t == 2 and n % 2 == 0 and 0 < n < NB:
                 spread_bb(n)
             if len(waiting) == 3:

@@ -43,16 +43,15 @@ def tile_blockdiagmnistconvertible_pa_kernel(tc, x, W1_words, W1_scales, b1, Wb,
         py_pool = ctx.enter_context(tc.psum_pool(name="py", bufs=3))
         ctx.enter_context(tc.manual_schedule())
 
-        bias_rows = consts.tile([P, P], BF16)
-        nc.vector.memset(bias_rows[:].bitcast(I32), 0)
+        b1_rows = consts.tile([P, P], BF16)
+        nc.vector.memset(b1_rows[:].bitcast(I32), 0)
         w1_planes = consts.tile([P, HID], U8, align_bytes=64)
         nc.vector.memset(w1_planes[:].bitcast(I32), 0)
         ident_f32 = consts.tile([P, P], F32)
         make_identity(nc, ident_f32[:])
         ident_bf = consts.tile([P, P], BF16)
         make_identity(nc, ident_bf[:])
-        nc.scalar.dma_start(out=bias_rows[0 : HID // P, :], in_=b1.rearrange("(j p) -> j p", p=P))
-        nc.scalar.dma_start(out=bias_rows[HID // P : 2 * HID // P, :], in_=bb.rearrange("(j p) -> j p", p=P))
+        nc.scalar.dma_start(out=b1_rows[0 : HID // P, :], in_=b1.rearrange("(j p) -> j p", p=P))
 
         x_sb = []
         for i in range(B_TILES):
@@ -82,9 +81,12 @@ def tile_blockdiagmnistconvertible_pa_kernel(tc, x, W1_words, W1_scales, b1, Wb,
                 in_=W1_scales[:, 4 * q : 4 * q + 4, :].bitcast(I32),
             )
         load_wb(0)
+        bb_rows = consts.tile([P, HID], BF16)
         for n in range(1, NB):
             load_w1(n)
             load_wb(n)
+            if n == 1:
+                nc.sync.dma_start(out=bb_rows[:], in_=bb.partition_broadcast(P))
 
         x_codes = consts.tile([P, X_PASSES, B], U32, align_bytes=64)
         x_planes = consts.tile([P, X_PASSES, B], U8, align_bytes=64)
@@ -99,7 +101,7 @@ def tile_blockdiagmnistconvertible_pa_kernel(tc, x, W1_words, W1_scales, b1, Wb,
             nc.scalar.copy(out=x_grouped[:].bitcast(F32), in_=px[:].rearrange("p g u b -> p g b u"))
             if i == B_TILES - 1:
                 pb = pw_pool.tile([P, P], BF16, tag="pw")
-                nc.tensor.transpose(pb[:], bias_rows[:], ident_bf[:])
+                nc.tensor.transpose(pb[:], b1_rows[:], ident_bf[:])
                 b1_cols = consts.tile([P, HID // P], F32)
                 nc.vector.tensor_copy(out=b1_cols[:], in_=pb[:, 0 : HID // P])
             for g in range(X_PASSES):
@@ -109,20 +111,6 @@ def tile_blockdiagmnistconvertible_pa_kernel(tc, x, W1_words, W1_scales, b1, Wb,
                     in_=x_grouped[:, g, :, :].rearrange("p b t -> p (b t)"),
                 )
 
-        bb_spread = {}
-
-        def spread_bb(n):
-            pb = pw_pool.tile([P, 2, 4, P], BF16, tag="pw")
-            for c in range(2):
-                for j in range(4):
-                    row = HID // P + (n + c) * BLK // P + j
-                    nc.tensor.matmul(pb[:, c, j, :], lhsT=ident_bf[:, row : row + 1].to_broadcast([P, P]), rhs=bias_rows[:], start=True, stop=True)
-            pair = consts.tile([P, 2, BLK], BF16, name="bb_spread%d" % n)
-            nc.scalar.copy(out=pair[:].rearrange("p c o -> p (c o)"), in_=pb[:].rearrange("p c j o -> p (c j o)"))
-            for c in range(2):
-                bb_spread[n + c] = pair[:, c, :]
-
-        spread_bb(0)
         wb_banks = {}
         grouped = {}
         h_plain = {}
@@ -136,7 +124,13 @@ def tile_blockdiagmnistconvertible_pa_kernel(tc, x, W1_words, W1_scales, b1, Wb,
                 pw = pw_pool.tile([P, 2, 4, P], BF16, tag="pw")
                 for a in range(4):
                     for c in range(2):
-                        nc.tensor.transpose(pw[:, c, a, :], wb_rows[n][:, 4 * half + a, c * P : (c + 1) * P], ident_bf[:])
+                        nc.tensor.matmul(
+                            pw[:, c, a, :],
+                            lhsT=wb_rows[n][:, 4 * half + a, c * P : (c + 1) * P],
+                            rhs=ident_bf[:],
+                            start=True,
+                            stop=True,
+                        )
                 wb_banks[n, half] = pw
 
         def copy_wb(n, half):
@@ -193,7 +187,7 @@ def tile_blockdiagmnistconvertible_pa_kernel(tc, x, W1_words, W1_scales, b1, Wb,
                 stop=True,
             )
             res = res_pool.tile([P, BLK], F32, name="res")
-            nc.vector.tensor_tensor(out=res[:], in0=py[:], in1=bb_spread[n], op=ADD)
+            nc.vector.tensor_tensor(out=res[:], in0=py[:], in1=bb_rows[:, n * BLK : (n + 1) * BLK], op=ADD)
             return res
 
         def relu_and_store(n, i, res):
@@ -224,8 +218,6 @@ def tile_blockdiagmnistconvertible_pa_kernel(tc, x, W1_words, W1_scales, b1, Wb,
                 waiting.append((m, i, second_product(m, i)))
             if t == 0 and 1 <= n <= NB:
                 quantise(n - 1)
-            if t == 2 and n % 2 == 0 and 0 < n < NB:
-                spread_bb(n)
             if len(waiting) == 3:
                 relu_and_store(*waiting.pop(0))
             if t == H_TILES - 1 and n < NB:

@@ -35,7 +35,7 @@ def tile_blockdiagmnistconvertible_pa_kernel(tc, x, W1_words, W1_scales, b1, Wb,
         consts = ctx.enter_context(tc.tile_pool(name="consts", bufs=1))
         w1_pool = ctx.enter_context(tc.tile_pool(name="w1", bufs=NB))
         wb_pool = ctx.enter_context(tc.tile_pool(name="wb", bufs=NB))
-        work = ctx.enter_context(tc.tile_pool(name="work", bufs=2))
+        work = ctx.enter_context(tc.tile_pool(name="work", bufs=3))
         quant = ctx.enter_context(tc.tile_pool(name="quant", bufs=4))
         res_pool = ctx.enter_context(tc.tile_pool(name="res", bufs=16))
         pw_pool = ctx.enter_context(tc.psum_pool(name="pw", bufs=2))
@@ -46,15 +46,25 @@ def tile_blockdiagmnistconvertible_pa_kernel(tc, x, W1_words, W1_scales, b1, Wb,
         b1_rows = consts.tile([P, P], BF16)
         nc.vector.memset(b1_rows[:].bitcast(I32), 0)
         w1_planes = consts.tile([P, HID], U8, align_bytes=64)
-        nc.vector.memset(w1_planes[:].bitcast(I32), 0)
+        nc.vector.memset(w1_planes[:, 0:BLK].bitcast(I32), 0)
+        nc.vector.memset(w1_planes[:, BLK:HID].bitcast(I32), 0)
         ident_f32 = consts.tile([P, P], F32)
         make_identity(nc, ident_f32[:])
         ident_bf = consts.tile([P, P], BF16)
         make_identity(nc, ident_bf[:])
         nc.scalar.dma_start(out=b1_rows[0 : HID // P, :], in_=b1.rearrange("(j p) -> j p", p=P))
 
+        def load_scales(lo, hi):
+            for q in range(4):
+                nc.sync.dma_start(
+                    out=w1_planes[32 * q : 32 * q + 4 * X_PASSES, lo:hi].bitcast(I32),
+                    in_=W1_scales[:, 4 * q : 4 * q + 4, lo:hi].bitcast(I32),
+                )
+
         x_sb = []
         for i in range(B_TILES):
+            if i == 2:
+                load_scales(0, BLK)
             x_rows = consts.tile([P, IN], BF16, name="x_rows%d" % i)
             nc.sync.dma_start(out=x_rows[:], in_=x[i * P : (i + 1) * P, :])
             x_sb.append(x_rows)
@@ -75,12 +85,8 @@ def tile_blockdiagmnistconvertible_pa_kernel(tc, x, W1_words, W1_scales, b1, Wb,
             nc.sync.dma_start(out=wb_rows[n][:], in_=half_rows.rearrange("(a q) c -> q a c", q=P))
 
         load_w1(0)
-        for q in range(4):
-            nc.sync.dma_start(
-                out=w1_planes[32 * q : 32 * q + 4 * X_PASSES, :].bitcast(I32),
-                in_=W1_scales[:, 4 * q : 4 * q + 4, :].bitcast(I32),
-            )
         load_wb(0)
+        load_scales(BLK, HID)
         bb_rows = consts.tile([P, HID], BF16)
         for n in range(1, NB):
             load_w1(n)
@@ -117,26 +123,25 @@ def tile_blockdiagmnistconvertible_pa_kernel(tc, x, W1_words, W1_scales, b1, Wb,
         codes = {}
         planes = {}
 
-        def transpose_wb(n):
-            if n > 0:
-                grouped[n] = work.tile([P, 2, BLK, PACK], BF16, name="grouped", align_bytes=64)
-            for half in range(2):
-                pw = pw_pool.tile([P, 2, 4, P], BF16, tag="pw")
-                for a in range(4):
-                    for c in range(2):
-                        nc.tensor.matmul(
-                            pw[:, c, a, :],
-                            lhsT=wb_rows[n][:, 4 * half + a, c * P : (c + 1) * P],
-                            rhs=ident_bf[:],
-                            start=True,
-                            stop=True,
-                        )
-                wb_banks[n, half] = pw
+        def transpose_wb(n, half):
+            pw = pw_pool.tile([P, 2 * P, 2, 2], BF16, tag="pw")
+            for a in range(4):
+                for c in range(2):
+                    nc.tensor.matmul(
+                        pw[:, 64 * a : 64 * (a + 1), c, :],
+                        lhsT=wb_rows[n][:, 4 * half + a, c * P : (c + 1) * P],
+                        rhs=ident_bf[:],
+                        start=True,
+                        stop=True,
+                    )
+            wb_banks[n, half] = pw
 
         def copy_wb(n, half):
+            if half == 0 and n > 0:
+                grouped[n] = work.tile([P, 2, BLK, PACK], BF16, name="grouped", align_bytes=64)
             nc.scalar.copy(
-                out=grouped[n][:, 1, half * 2 * P : (half + 1) * 2 * P, :].bitcast(F32),
-                in_=wb_banks[n, half][:].bitcast(F32).rearrange("p c a w -> p (a w) c"),
+                out=grouped[n][:, 1, half * 2 * P : (half + 1) * 2 * P, :].rearrange("p o t -> p (o t)").bitcast(F32),
+                in_=wb_banks[n, half][:].rearrange("p o c u -> p (o c u)").bitcast(F32),
             )
 
         def first_product(n, t, cols):
@@ -191,7 +196,9 @@ def tile_blockdiagmnistconvertible_pa_kernel(tc, x, W1_words, W1_scales, b1, Wb,
             return res
 
         def relu_and_store(n, i, res):
-            if i >= 2:
+            if n == NB - 1 and i % 2 == 1:
+                nc.vector.tensor_scalar(out=res[:], in0=res[:], scalar1=0.0, scalar2=None, op0=MAX)
+            elif n < NB - 1 and i in (1, 2):
                 nc.gpsimd.tensor_scalar(out=res[:], in0=res[:], scalar1=FLT_MAX, scalar2=0.0, op0=MIN, op1=MAX)
             else:
                 nc.scalar.activation(out=res[:], in_=res[:], func=RELU)
@@ -211,18 +218,22 @@ def tile_blockdiagmnistconvertible_pa_kernel(tc, x, W1_words, W1_scales, b1, Wb,
                         regroup_h(0, halves[0])
             elif H_TILES <= step < NB * H_TILES:
                 first_product(n, t, slice(0, B))
+            if t == H_TILES - 1 and n < NB:
+                copy_wb(n, 0)
             if t == 0 and 1 <= n <= NB:
+                if n > 1:
+                    copy_wb(n - 1, 1)
                 regroup_h(n - 1, halves[1] if n == 1 else slice(0, B))
             if step >= LAG:
                 m, i = divmod(step - LAG, B_TILES)
                 waiting.append((m, i, second_product(m, i)))
             if t == 0 and 1 <= n <= NB:
                 quantise(n - 1)
-            if len(waiting) == 3:
+            if len(waiting) == 4:
                 relu_and_store(*waiting.pop(0))
-            if t == H_TILES - 1 and n < NB:
-                transpose_wb(n)
-                copy_wb(n, 0)
-                copy_wb(n, 1)
+            if t >= H_TILES - 2 and n < NB:
+                transpose_wb(n, t - (H_TILES - 2))
+                if n == 0 and t == H_TILES - 1:
+                    copy_wb(0, 1)
         for last in waiting:
             relu_and_store(*last)

from contextlib import ExitStack

import concourse.mybir as mybir
from concourse.masks import make_identity

F32 = mybir.dt.float32
BF16 = mybir.dt.bfloat16
I32 = mybir.dt.int32
U32 = mybir.dt.uint32
U8 = mybir.dt.uint8
FP8X4 = mybir.dt.float8_e4m3fn_x4
RELU = mybir.ActivationFunctionType.Relu
ADD = mybir.AluOpType.add
MAX = mybir.AluOpType.max
MIN = mybir.AluOpType.min
FLT_MAX = 3.4028235e38

P = 128
PACK = 4
K_PASS = P * PACK
B, IN, HID, BLK = 512, 1024, 4096, 512
NB = HID // BLK
X_PASSES = IN // K_PASS
B_TILES = B // P
H_TILES = BLK // P
HALF = B // 2
LAG = 7

FLOPS = 2 * B * IN * HID + 2 * B * BLK * HID


def tile_blockdiagmnistconvertible_pa_kernel(tc, x, W1_words, W1_scales, b1, Wb, bb, out):
    nc = tc.nc
    with ExitStack() as ctx:
        consts = ctx.enter_context(tc.tile_pool(name="consts", bufs=1))
        w1_pool = ctx.enter_context(tc.tile_pool(name="w1", bufs=NB))
        wb_pool = ctx.enter_context(tc.tile_pool(name="wb", bufs=NB))
        work = ctx.enter_context(tc.tile_pool(name="work", bufs=3))
        quant = ctx.enter_context(tc.tile_pool(name="quant", bufs=4))
        res_pool = ctx.enter_context(tc.tile_pool(name="res", bufs=16))
        pw_pool = ctx.enter_context(tc.psum_pool(name="pw", bufs=2))
        ph_pool = ctx.enter_context(tc.psum_pool(name="ph", bufs=3))
        py_pool = ctx.enter_context(tc.psum_pool(name="py", bufs=3))
        ctx.enter_context(tc.manual_schedule())

        b1_rows = consts.tile([P, P], BF16)
        nc.vector.memset(b1_rows[:].bitcast(I32), 0)
        w1_planes = consts.tile([P, HID], U8, align_bytes=64)
        nc.vector.memset(w1_planes[:, 0:BLK].bitcast(I32), 0)
        nc.vector.memset(w1_planes[:, BLK:HID].bitcast(I32), 0)
        ident_f32 = consts.tile([P, P], F32)
        make_identity(nc, ident_f32[:])
        ident_bf = consts.tile([P, P], BF16)
        make_identity(nc, ident_bf[:])
        nc.scalar.dma_start(out=b1_rows[0 : HID // P, :], in_=b1.rearrange("(j p) -> j p", p=P))

        def load_scales(lo, hi):
            for q in range(4):
                nc.sync.dma_start(
                    out=w1_planes[32 * q : 32 * q + 4 * X_PASSES, lo:hi].bitcast(I32),
                    in_=W1_scales[:, 4 * q : 4 * q + 4, lo:hi].bitcast(I32),
                )

        x_sb = []
        for i in range(B_TILES):
            if i == 2:
                load_scales(0, BLK)
            x_rows = consts.tile([P, IN], BF16, name="x_rows%d" % i)
            nc.sync.dma_start(out=x_rows[:], in_=x[i * P : (i + 1) * P, :])
            x_sb.append(x_rows)

        w1_words = {}
        wb_rows = {}

        def load_w1(n):
            w1_words[n] = w1_pool.tile([P, X_PASSES, BLK], U32, name="w1_words", align_bytes=64)
            nc.sync.dma_start(
                out=w1_words[n][:].bitcast(I32),
                in_=W1_words.rearrange("g p n t -> p g (n t)")[:, :, n * BLK * PACK : (n + 1) * BLK * PACK].bitcast(I32),
            )

        def load_wb(n):
            wb_rows[n] = wb_pool.tile([P, 2 * BLK // P, BLK // 2], BF16, name="wb_rows")
            half_rows = Wb[n].rearrange("o (u c) -> (o u) c", u=2)
            nc.sync.dma_start(out=wb_rows[n][:], in_=half_rows.rearrange("(a q) c -> q a c", q=P))

        load_w1(0)
        load_wb(0)
        load_scales(BLK, HID)
        bb_rows = consts.tile([P, HID], BF16)
        for n in range(1, NB):
            load_w1(n)
            load_wb(n)
            if n == 1:
                nc.sync.dma_start(out=bb_rows[:], in_=bb.partition_broadcast(P))

        x_codes = consts.tile([P, X_PASSES, B], U32, align_bytes=64)
        x_planes = consts.tile([P, X_PASSES, B], U8, align_bytes=64)
        for i in range(B_TILES):
            rows = slice(i * P, (i + 1) * P)
            px = py_pool.tile([P, X_PASSES, 2, P], F32, tag="py")
            x_words = x_sb[i][:].bitcast(F32)
            for g in range(X_PASSES):
                for u in range(2):
                    nc.tensor.transpose(px[:, g, u, :], x_words[:, 256 * g + u : 256 * (g + 1) : 2], ident_f32[:])
            x_grouped = consts.tile([P, X_PASSES, P, PACK], BF16, name="x_grouped%d" % i, align_bytes=64)
            nc.scalar.copy(out=x_grouped[:].bitcast(F32), in_=px[:].rearrange("p g u b -> p g b u"))
            if i == B_TILES - 1:
                pb = pw_pool.tile([P, P], BF16, tag="pw")
                nc.tensor.transpose(pb[:], b1_rows[:], ident_bf[:])
                b1_cols = consts.tile([P, HID // P], F32)
                nc.vector.tensor_copy(out=b1_cols[:], in_=pb[:, 0 : HID // P])
            for g in range(X_PASSES):
                nc.vector.quantize_mx(
                    out=x_codes[:, g, rows].bitcast(FP8X4),
                    scales=x_planes[:, g, rows],
                    in_=x_grouped[:, g, :, :].rearrange("p b t -> p (b t)"),
                )

        wb_banks = {}
        grouped = {}
        h_plain = {}
        codes = {}
        planes = {}

        def transpose_wb(n, half):
            pw = pw_pool.tile([P, 2 * P, 2, 2], BF16, tag="pw")
            for a in range(4):
                for c in range(2):
                    nc.tensor.matmul(
                        pw[:, 64 * a : 64 * (a + 1), c, :],
                        lhsT=wb_rows[n][:, 4 * half + a, c * P : (c + 1) * P],
                        rhs=ident_bf[:],
                        start=True,
                        stop=True,
                    )
            wb_banks[n, half] = pw

        def copy_wb(n, half):
            if half == 0 and n > 0:
                grouped[n] = work.tile([P, 2, BLK, PACK], BF16, name="grouped", align_bytes=64)
            nc.scalar.copy(
                out=grouped[n][:, 1, half * 2 * P : (half + 1) * 2 * P, :].rearrange("p o t -> p (o t)").bitcast(F32),
                in_=wb_banks[n, half][:].rearrange("p o c u -> p (o c u)").bitcast(F32),
            )

        def first_product(n, t, cols):
            hidden = slice(t * P, (t + 1) * P)
            ph = ph_pool.tile([P, B], F32, tag="ph")
            width = cols.stop - cols.start
            for g in range(X_PASSES):
                nc.tensor.matmul_mx(
                    out=ph[:, 0:width],
                    lhsT=w1_words[n][:, g, hidden].bitcast(FP8X4),
                    lhsT_scale=w1_planes[4 * g : P, n * BLK + t * P : n * BLK + (t + 1) * P],
                    rhs=x_codes[:, g, cols].bitcast(FP8X4),
                    rhs_scale=x_planes[:, g, cols],
                    start=(g == 0),
                    stop=(g == X_PASSES - 1),
                )
            j = n * H_TILES + t
            place = 2 * (t % 2) + t // 2
            nc.scalar.activation(out=h_plain[n][:, place, cols], in_=ph[:, 0:width], func=RELU, bias=b1_cols[:, j : j + 1], scale=1.0)

        halves = [slice(0, HALF), slice(HALF, B)]

        def regroup_h(n, cols):
            nc.vector.tensor_copy(
                out=grouped[n][:, 0, cols, :].rearrange("p (c i) t -> p c t i", i=4),
                in_=h_plain[n][:, :, cols].rearrange("p t (c i) -> p c t i", i=4),
            )

        def quantise(n):
            codes[n] = quant.tile([P, 2, BLK], U32, name="codes", align_bytes=64)
            planes[n] = quant.tile([P, 2, BLK], U8, name="planes", align_bytes=64)
            nc.vector.quantize_mx(
                out=codes[n][:].rearrange("p s o -> p (s o)").bitcast(FP8X4),
                scales=planes[n][:].rearrange("p s o -> p (s o)"),
                in_=grouped[n][:].rearrange("p s o t -> p (s o t)"),
            )

        def second_product(n, i):
            rows = slice(i * P, (i + 1) * P)
            py = py_pool.tile([P, BLK], F32, tag="py")
            nc.tensor.matmul_mx(
                out=py[:],
                lhsT=codes[n][:, 0, rows].bitcast(FP8X4),
                lhsT_scale=planes[n][:, 0, rows],
                rhs=codes[n][:, 1, :].bitcast(FP8X4),
                rhs_scale=planes[n][:, 1, :],
                start=True,
                stop=True,
            )
            res = res_pool.tile([P, BLK], F32, name="res")
            nc.vector.tensor_tensor(out=res[:], in0=py[:], in1=bb_rows[:, n * BLK : (n + 1) * BLK], op=ADD)
            return res

        def relu_and_store(n, i, res):
            if n == NB - 1 and i % 2 == 1:
                nc.vector.tensor_scalar(out=res[:], in0=res[:], scalar1=0.0, scalar2=None, op0=MAX)
            elif n < NB - 1 and i in (1, 2):
                nc.gpsimd.tensor_scalar(out=res[:], in0=res[:], scalar1=FLT_MAX, scalar2=0.0, op0=MIN, op1=MAX)
            else:
                nc.scalar.activation(out=res[:], in_=res[:], func=RELU)
            nc.sync.dma_start(out=out[i * P : (i + 1) * P, n * BLK : (n + 1) * BLK], in_=res[:])

        waiting = []
        for step in range(NB * H_TILES + LAG):
            n, t = divmod(step, H_TILES)
            if t == 0 and n < NB:
                h_plain[n] = work.tile([P, H_TILES, B], BF16, name="h_plain")
            if step == 0:
                for half in range(2):
                    for first in range(H_TILES):
                        first_product(0, first, halves[half])
                    if half == 0:
                        grouped[0] = work.tile([P, 2, BLK, PACK], BF16, name="grouped", align_bytes=64)
                        regroup_h(0, halves[0])
            elif H_TILES <= step < NB * H_TILES:
                first_product(n, t, slice(0, B))
            if t == H_TILES - 1 and n < NB:
                copy_wb(n, 0)
            if t == 0 and 1 <= n <= NB:
                if n > 1:
                    copy_wb(n - 1, 1)
                regroup_h(n - 1, halves[1] if n == 1 else slice(0, B))
            if step >= LAG:
                m, i = divmod(step - LAG, B_TILES)
                waiting.append((m, i, second_product(m, i)))
            if t == 0 and 1 <= n <= NB:
                quantise(n - 1)
            if len(waiting) == 4:
                relu_and_store(*waiting.pop(0))
            if t >= H_TILES - 2 and n < NB:
                transpose_wb(n, t - (H_TILES - 2))
                if n == 0 and t == H_TILES - 1:
                    copy_wb(0, 1)
        for last in waiting:
            relu_and_store(*last)
